import numpy as np
import ml_dtypes


def mxq(x, axis, fmt="e4m3"):
    dtype, down = {"e4m3": (ml_dtypes.float8_e4m3fn, 7), "e5m2": (ml_dtypes.float8_e5m2, 14)}[fmt]
    v = np.moveaxis(np.asarray(x, np.float32).astype(ml_dtypes.bfloat16).astype(np.float64), axis, -1)
    blocks = v.reshape(v.shape[:-1] + (-1, 32))
    amax = np.abs(blocks).max(-1, keepdims=True)
    byte = np.maximum(np.where(amax > 0, np.frexp(amax)[1] - 1 + 127, 0) - down, 1)
    scale = np.exp2(byte - 127.0)
    codes = (blocks / scale).astype(np.float32).astype(dtype).astype(np.float64)
    return np.moveaxis((codes * scale).reshape(v.shape), -1, axis)


WIDE = False


def mx_kscale(k):
    if not WIDE:
        return np.ones(k)
    levels = np.array([10, -10, 5, -5, 0])
    a = np.random.permutation(np.resize(levels, k // 512 * 4)).reshape(k // 512, 4)
    idx = np.arange(k)
    return np.exp2(a[idx // 512, idx % 128 // 32])


BF16 = ml_dtypes.bfloat16


def bf(x):
    return np.asarray(x, np.float32).astype(BF16)


def f64(x):
    return np.asarray(x).astype(np.float64)


B, D_IN, D_OUT = 4096, 1024, 256


def sigmoid(v):
    return 1.0 / (1.0 + np.exp(-v))


def setup_inputs():
    s = mx_kscale(D_IN)
    w = lambda: bf(np.random.standard_normal((D_IN, D_OUT)) / np.sqrt(D_IN) / s[:, None])
    b = lambda: bf(np.random.standard_normal(D_OUT) * 0.5)
    return {"x": bf(np.random.standard_normal((B, D_IN)) * s),
            "Wxi": w(), "bxi": b(),
            "Wxc": w(), "bxc": b(),
            "Wxo": w(), "bxo": b()}


def reference(x, Wxi, bxi, Wxc, bxc, Wxo, bxo):
    xq = mxq(f64(x), 1, "e4m3")
    gi = (xq @ mxq(f64(Wxi), 0, "e4m3")) + f64(bxi)
    gc = (xq @ mxq(f64(Wxc), 0, "e4m3")) + f64(bxc)
    go = (xq @ mxq(f64(Wxo), 0, "e4m3")) + f64(bxo)
    i = sigmoid(gi)
    c = np.tanh(gc)
    o = sigmoid(go)
    new_state = c * i
    return np.tanh(new_state) * o

@@ -1,0 +1,245 @@
+from contextlib import ExitStack
+
+import concourse.mybir as mybir
+from concourse.masks import make_identity
+
+F32 = mybir.dt.float32
+BF16 = mybir.dt.bfloat16
+U32 = mybir.dt.uint32
+U8 = mybir.dt.uint8
+FP8X4 = mybir.dt.float8_e4m3fn_x4
+ACT = mybir.ActivationFunctionType
+MULT = mybir.AluOpType.mult
+
+BATCH, D_IN, D_OUT = 4096, 1024, 256
+FLOPS = 2 * BATCH * D_IN * 3 * D_OUT
+
+P = 128
+PACK = 4
+K_PASS = P * PACK
+PASSES = D_IN // K_PASS
+GROUP = 512
+ROW_TILES = GROUP // P
+GROUPS = BATCH // GROUP
+HALVES = D_OUT // P
+PAIR_WORDS = D_IN // 2
+GATES = ("i", "c", "o")
+
+
+def tile_lstm_pa_t_kernel(tc, x, Wxi, bxi, Wxc, bxc, Wxo, bxo, out):
+    nc = tc.nc
+    weights = {"i": Wxi, "c": Wxc, "o": Wxo}
+    biases = {"i": bxi, "c": bxc, "o": bxo}
+    functions = {"i": ACT.Sigmoid, "c": ACT.Tanh, "o": ACT.Sigmoid}
+
+    with ExitStack() as ctx:
+        const = ctx.enter_context(tc.tile_pool(name="const", bufs=1))
+        x_pool = ctx.enter_context(tc.tile_pool(name="x_pool", bufs=GROUPS))
+        operand = ctx.enter_context(tc.tile_pool(name="operand", bufs=2))
+        values = ctx.enter_context(tc.tile_pool(name="values", bufs=2 * HALVES))
+        result = ctx.enter_context(tc.tile_pool(name="result", bufs=2))
+        gate_psum = ctx.enter_context(tc.psum_pool(name="gate_psum", bufs=4))
+        turn_psum = ctx.enter_context(tc.psum_pool(name="turn_psum", bufs=4))
+        ctx.enter_context(tc.manual_schedule())
+
+        identity = const.tile([P, P], F32)
+        make_identity(nc, identity[:])
+
+        w_raw = {}
+        x_sb = {}
+
+        def load_weight(gate):
+            w_raw[gate] = const.tile([P, PASSES * PACK * D_OUT], BF16, name="w_raw_" + gate)
+            nc.sync.dma_start(
+                out=w_raw[gate][:].rearrange("p (s r) -> p s r", s=2 * PASSES),
+                in_=weights[gate].rearrange("(s p e) c -> p s (e c)", p=P, e=2),
+            )
+
+        def load_x(n):
+            x_sb[n] = x_pool.tile([P, ROW_TILES * D_IN], BF16, name="x_sb", tag="x_sb")
+            nc.sync.dma_start(
+                out=x_sb[n][:],
+                in_=x[n * GROUP : (n + 1) * GROUP, :].rearrange("(r j) k -> r (j k)", j=ROW_TILES),
+            )
+
+        load_weight("i")
+        load_weight("c")
+        load_x(0)
+        load_weight("o")
+        for n in range(1, GROUPS):
+            load_x(n)
+
+        bias_rows = const.tile([P, P], BF16)
+        nc.vector.memset(bias_rows[:], 0.0)
+        for row, gate in enumerate(GATES):
+            nc.scalar.dma_start(
+                out=bias_rows[HALVES * row : HALVES * (row + 1), :],
+                in_=biases[gate].rearrange("(h d) -> h d", h=HALVES),
+            )
+        bias_rows_f32 = const.tile([P, P], F32)
+        nc.vector.tensor_copy(out=bias_rows_f32[:], in_=bias_rows[:])
+        bias_turned = turn_psum.tile([P, GROUP], F32, name="bias_turned", tag="turned")
+        nc.tensor.transpose(bias_turned[:, 0:P], bias_rows_f32[:], identity[:])
+        bias_cols = const.tile([P, len(GATES) * HALVES], F32)
+        nc.vector.tensor_copy(out=bias_cols[:], in_=bias_turned[:, 0 : len(GATES) * HALVES])
+
+        w_codes = {}
+        w_scales = {}
+
+        def prepare_weight(gate):
+            grouped = const.tile(
+                [P, PASSES * D_OUT * PACK], BF16, name="w_grouped_" + gate, align_bytes=64
+            )
+            nc.vector.tensor_copy(
+                out=grouped[:].rearrange("p (g c t) -> p g c t", g=PASSES, t=PACK),
+                in_=w_raw[gate][:].rearrange("p (g t c) -> p g c t", g=PASSES, t=PACK),
+            )
+            w_codes[gate] = const.tile(
+                [P, PASSES * D_OUT], U32, name="w_codes_" + gate, align_bytes=64
+            )
+            w_scales[gate] = const.tile(
+                [P, PASSES * D_OUT], U8, name="w_scales_" + gate, align_bytes=64
+            )
+            nc.vector.quantize_mx(
+                out=w_codes[gate][:].bitcast(FP8X4), scales=w_scales[gate][:], in_=grouped[:]
+            )
+
+        x_grouped = {}
+        x_codes = {}
+        x_scales = {}
+
+        def transpose_x(n):
+            words = x_sb[n][:].bitcast(F32)
+            x_grouped[n] = operand.tile(
+                [P, PASSES * GROUP * PACK], BF16, name="x_grouped", tag="x_grouped", align_bytes=64
+            )
+            grouped_words = x_grouped[n][:].bitcast(F32)
+            for g in range(PASSES):
+                for first in range(0, ROW_TILES, 2):
+                    turned = turn_psum.tile([P, GROUP], F32, name="x_turned", tag="turned")
+                    for u in range(2):
+                        for j in (first, first + 1):
+                            start = j * PAIR_WORDS + (2 * g + u) * P
+                            nc.tensor.transpose(
+                                turned[:, (2 * u + j - first) * P : (2 * u + j - first + 1) * P],
+                                words[:, start : start + P],
+                                identity[:],
+                            )
+                    start = (g * GROUP + first * P) * 2
+                    last = g == PASSES - 1 and first == ROW_TILES - 2
+                    copy = nc.scalar.copy if last else nc.vector.tensor_copy
+                    copy(
+                        out=grouped_words[:, start : start + GROUP].rearrange(
+                            "p (c u) -> p c u", u=2
+                        ),
+                        in_=turned[:].rearrange("p (u c) -> p c u", u=2),
+                    )
+
+        def quantise_x(n):
+            x_codes[n] = operand.tile(
+                [P, PASSES * GROUP], U32, name="x_codes", tag="x_codes", align_bytes=64
+            )
+            x_scales[n] = operand.tile(
+                [P, PASSES * GROUP], U8, name="x_scales", tag="x_scales", align_bytes=64
+            )
+            for g in range(PASSES):
+                cols = slice(g * GROUP, (g + 1) * GROUP)
+                nc.vector.quantize_mx(
+                    out=x_codes[n][:, cols].bitcast(FP8X4),
+                    scales=x_scales[n][:, cols],
+                    in_=x_grouped[n][:, g * GROUP * PACK : (g + 1) * GROUP * PACK],
+                )
+
+        def gate_value(n, gate, half):
+            acc = gate_psum.tile([P, GROUP], F32, name="acc", tag="acc")
+            for g in range(PASSES):
+                w_cols = slice(g * D_OUT + half * P, g * D_OUT + (half + 1) * P)
+                x_cols = slice(g * GROUP, (g + 1) * GROUP)
+                nc.tensor.matmul_mx(
+                    out=acc[:],
+                    lhsT=w_codes[gate][:, w_cols].bitcast(FP8X4),
+                    lhsT_scale=w_scales[gate][:, w_cols],
+                    rhs=x_codes[n][:, x_cols].bitcast(FP8X4),
+                    rhs_scale=x_scales[n][:, x_cols],
+                    start=(g == 0),
+                    stop=(g == PASSES - 1),
+                )
+            value = values.tile([P, GROUP], F32, name="gate_" + gate, tag="gate_" + gate)
+            column = GATES.index(gate) * HALVES + half
+            nc.scalar.activation(
+                out=value[:],
+                in_=acc[:],
+                func=functions[gate],
+                bias=bias_cols[:, column : column + 1],
+                scale=1.0,
+            )
+            return value
+
+        o_value = {}
+        tanh_state = {}
+
+        def gates(n):
+            state = []
+            for half in range(HALVES):
+                i_value = gate_value(n, "i", half)
+                c_value = gate_value(n, "c", half)
+                state.append(values.tile([P, GROUP], F32, name="state", tag="state"))
+                nc.gpsimd.tensor_tensor(
+                    out=state[half][:], in0=c_value[:], in1=i_value[:], op=MULT
+                )
+            for half in range(HALVES):
+                o_value[n, half] = gate_value(n, "o", half)
+                tanh_state[n, half] = values.tile(
+                    [P, GROUP], F32, name="tanh_state", tag="tanh_state"
+                )
+                nc.scalar.activation(
+                    out=tanh_state[n, half][:], in_=state[half][:], func=ACT.Tanh
+                )
+
+        hidden = {}
+
+        def output_product(n):
+            for half in range(HALVES):
+                hidden[n, half] = values.tile([P, GROUP], F32, name="hidden", tag="hidden")
+                nc.vector.tensor_tensor(
+                    out=hidden[n, half][:],
+                    in0=tanh_state[n, half][:],
+                    in1=o_value[n, half][:],
+                    op=MULT,
+                )
+
+        def store_output(n):
+            rows = result.tile([P, ROW_TILES * D_OUT], F32, name="rows", tag="rows")
+            for first in range(0, ROW_TILES, 2):
+                turned = turn_psum.tile([P, GROUP], F32, name="out_turned", tag="turned")
+                for j in (first, first + 1):
+                    for half in range(HALVES):
+                        start = (j - first) * D_OUT + half * P
+                        nc.tensor.transpose(
+                            turned[:, start : start + P],
+                            hidden[n, half][:, j * P : (j + 1) * P],
+                            identity[:],
+                        )
+                nc.vector.tensor_copy(
+                    out=rows[:, first * D_OUT : (first + 2) * D_OUT], in_=turned[:]
+                )
+            nc.sync.dma_start(
+                out=out[n * GROUP : (n + 1) * GROUP, :].rearrange("(r j) d -> r (j d)", j=ROW_TILES),
+                in_=rows[:],
+            )
+
+        prepare_weight("i")
+        prepare_weight("c")
+        transpose_x(0)
+        quantise_x(0)
+        prepare_weight("o")
+        for n in range(GROUPS + 2):
+            if n + 1 < GROUPS:
+                transpose_x(n + 1)
+                quantise_x(n + 1)
+            if 0 <= n - 1 < GROUPS:
+                output_product(n - 1)
+            if 0 <= n - 2 < GROUPS:
+                store_output(n - 2)
+            if n < GROUPS:
+                gates(n)

@@ -22,7 +22,7 @@ GROUP = 512
 ROW_TILES = GROUP // P
 GROUPS = BATCH // GROUP
 HALVES = D_OUT // P
-PAIR_WORDS = D_IN // 2
+PAIR_WORDS = K_PASS // 2
 GATES = ("i", "c", "o")
 
 
@@ -34,16 +34,18 @@ def tile_lstm_pa_t_kernel(tc, x, Wxi, bxi, Wxc, bxc, Wxo, bxo, out):
 
     with ExitStack() as ctx:
         const = ctx.enter_context(tc.tile_pool(name="const", bufs=1))
-        x_pool = ctx.enter_context(tc.tile_pool(name="x_pool", bufs=GROUPS))
+        x_pool = ctx.enter_context(tc.tile_pool(name="x_pool", bufs=GROUPS * PASSES))
         operand = ctx.enter_context(tc.tile_pool(name="operand", bufs=2))
         values = ctx.enter_context(tc.tile_pool(name="values", bufs=2 * HALVES))
-        result = ctx.enter_context(tc.tile_pool(name="result", bufs=2))
+        result = ctx.enter_context(tc.tile_pool(name="result", bufs=4))
         gate_psum = ctx.enter_context(tc.psum_pool(name="gate_psum", bufs=4))
         turn_psum = ctx.enter_context(tc.psum_pool(name="turn_psum", bufs=4))
         ctx.enter_context(tc.manual_schedule())
 
         identity = const.tile([P, P], F32)
         make_identity(nc, identity[:])
+        identity_bf16 = const.tile([P, P], BF16)
+        make_identity(nc, identity_bf16[:])
 
         w_raw = {}
         x_sb = {}
@@ -56,44 +58,50 @@ def tile_lstm_pa_t_kernel(tc, x, Wxi, bxi, Wxc, bxc, Wxo, bxo, out):
             )
 
         def load_x(n):
-            x_sb[n] = x_pool.tile([P, ROW_TILES * D_IN], BF16, name="x_sb", tag="x_sb")
-            nc.sync.dma_start(
-                out=x_sb[n][:],
-                in_=x[n * GROUP : (n + 1) * GROUP, :].rearrange("(r j) k -> r (j k)", j=ROW_TILES),
-            )
-
-        load_weight("i")
-        load_weight("c")
-        load_x(0)
-        load_weight("o")
-        for n in range(1, GROUPS):
-            load_x(n)
+            for g in range(PASSES):
+                x_sb[n, g] = x_pool.tile([P, ROW_TILES * K_PASS], BF16, name="x_sb", tag="x_sb")
+                nc.sync.dma_start(
+                    out=x_sb[n, g][:].rearrange("r (j k) -> r j k", j=ROW_TILES),
+                    in_=x[n * GROUP : (n + 1) * GROUP, g * K_PASS : (g + 1) * K_PASS].rearrange(
+                        "(r j) k -> r j k", j=ROW_TILES
+                    ),
+                )
 
         bias_rows = const.tile([P, P], BF16)
         nc.vector.memset(bias_rows[:], 0.0)
+
+        for gate in GATES:
+            load_weight(gate)
+        load_x(0)
         for row, gate in enumerate(GATES):
-            nc.scalar.dma_start(
+            nc.sync.dma_start(
                 out=bias_rows[HALVES * row : HALVES * (row + 1), :],
                 in_=biases[gate].rearrange("(h d) -> h d", h=HALVES),
             )
-        bias_rows_f32 = const.tile([P, P], F32)
-        nc.vector.tensor_copy(out=bias_rows_f32[:], in_=bias_rows[:])
-        bias_turned = turn_psum.tile([P, GROUP], F32, name="bias_turned", tag="turned")
-        nc.tensor.transpose(bias_turned[:, 0:P], bias_rows_f32[:], identity[:])
-        bias_cols = const.tile([P, len(GATES) * HALVES], F32)
-        nc.vector.tensor_copy(out=bias_cols[:], in_=bias_turned[:, 0 : len(GATES) * HALVES])
+        for n in range(1, GROUPS):
+            load_x(n)
 
+        bias_cols = const.tile([P, len(GATES) * HALVES], F32)
+
+        def turn_biases():
+            bias_turned = turn_psum.tile([P, P], BF16, name="bias_turned", tag="turned")
+            nc.tensor.transpose(bias_turned[:], bias_rows[:], identity_bf16[:])
+            nc.scalar.copy(out=bias_cols[:], in_=bias_turned[:, 0 : len(GATES) * HALVES])
+
+        w_grouped = {}
         w_codes = {}
         w_scales = {}
 
-        def prepare_weight(gate):
-            grouped = const.tile(
+        def regroup_weight(gate, copy):
+            w_grouped[gate] = const.tile(
                 [P, PASSES * D_OUT * PACK], BF16, name="w_grouped_" + gate, align_bytes=64
             )
-            nc.vector.tensor_copy(
-                out=grouped[:].rearrange("p (g c t) -> p g c t", g=PASSES, t=PACK),
+            copy(
+                out=w_grouped[gate][:].rearrange("p (g c t) -> p g c t", g=PASSES, t=PACK),
                 in_=w_raw[gate][:].rearrange("p (g t c) -> p g c t", g=PASSES, t=PACK),
             )
+
+        def quantise_weight(gate):
             w_codes[gate] = const.tile(
                 [P, PASSES * D_OUT], U32, name="w_codes_" + gate, align_bytes=64
             )
@@ -101,7 +109,9 @@ def tile_lstm_pa_t_kernel(tc, x, Wxi, bxi, Wxc, bxc, Wxo, bxo, out):
                 [P, PASSES * D_OUT], U8, name="w_scales_" + gate, align_bytes=64
             )
             nc.vector.quantize_mx(
-                out=w_codes[gate][:].bitcast(FP8X4), scales=w_scales[gate][:], in_=grouped[:]
+                out=w_codes[gate][:].bitcast(FP8X4),
+                scales=w_scales[gate][:],
+                in_=w_grouped[gate][:],
             )
 
         x_grouped = {}
@@ -109,17 +119,17 @@ def tile_lstm_pa_t_kernel(tc, x, Wxi, bxi, Wxc, bxc, Wxo, bxo, out):
         x_scales = {}
 
         def transpose_x(n):
-            words = x_sb[n][:].bitcast(F32)
             x_grouped[n] = operand.tile(
                 [P, PASSES * GROUP * PACK], BF16, name="x_grouped", tag="x_grouped", align_bytes=64
             )
             grouped_words = x_grouped[n][:].bitcast(F32)
             for g in range(PASSES):
+                words = x_sb[n, g][:].bitcast(F32)
                 for first in range(0, ROW_TILES, 2):
                     turned = turn_psum.tile([P, GROUP], F32, name="x_turned", tag="turned")
                     for u in range(2):
                         for j in (first, first + 1):
-                            start = j * PAIR_WORDS + (2 * g + u) * P
+                            start = j * PAIR_WORDS + u * P
                             nc.tensor.transpose(
                                 turned[:, (2 * u + j - first) * P : (2 * u + j - first + 1) * P],
                                 words[:, start : start + P],
@@ -201,7 +211,8 @@ def tile_lstm_pa_t_kernel(tc, x, Wxi, bxi, Wxc, bxc, Wxo, bxo, out):
         def output_product(n):
             for half in range(HALVES):
                 hidden[n, half] = values.tile([P, GROUP], F32, name="hidden", tag="hidden")
-                nc.vector.tensor_tensor(
+                engine = nc.vector if half == HALVES - 1 else nc.gpsimd
+                engine.tensor_tensor(
                     out=hidden[n, half][:],
                     in0=tanh_state[n, half][:],
                     in1=o_value[n, half][:],
@@ -209,7 +220,9 @@ def tile_lstm_pa_t_kernel(tc, x, Wxi, bxi, Wxc, bxc, Wxo, bxo, out):
                 )
 
         def store_output(n):
-            rows = result.tile([P, ROW_TILES * D_OUT], F32, name="rows", tag="rows")
+            group_rows = out[n * GROUP : (n + 1) * GROUP, :].rearrange(
+                "(r j) d -> r j d", j=ROW_TILES
+            )
             for first in range(0, ROW_TILES, 2):
                 turned = turn_psum.tile([P, GROUP], F32, name="out_turned", tag="turned")
                 for j in (first, first + 1):
@@ -220,19 +233,22 @@ def tile_lstm_pa_t_kernel(tc, x, Wxi, bxi, Wxc, bxc, Wxo, bxo, out):
                             hidden[n, half][:, j * P : (j + 1) * P],
                             identity[:],
                         )
-                nc.vector.tensor_copy(
-                    out=rows[:, first * D_OUT : (first + 2) * D_OUT], in_=turned[:]
+                rows = result.tile([P, 2 * D_OUT], F32, name="rows", tag="rows")
+                nc.vector.tensor_copy(out=rows[:], in_=turned[:])
+                nc.sync.dma_start(
+                    out=group_rows[:, first : first + 2, :],
+                    in_=rows[:].rearrange("r (j d) -> r j d", j=2),
                 )
-            nc.sync.dma_start(
-                out=out[n * GROUP : (n + 1) * GROUP, :].rearrange("(r j) d -> r (j d)", j=ROW_TILES),
-                in_=rows[:],
-            )
 
-        prepare_weight("i")
-        prepare_weight("c")
+        regroup_weight("i", nc.vector.tensor_copy)
+        regroup_weight("c", nc.vector.tensor_copy)
+        regroup_weight("o", nc.scalar.copy)
+        quantise_weight("i")
+        quantise_weight("c")
         transpose_x(0)
+        turn_biases()
         quantise_x(0)
-        prepare_weight("o")
+        quantise_weight("o")
         for n in range(GROUPS + 2):
             if n + 1 < GROUPS:
                 transpose_x(n + 1)

@@ -185,25 +185,27 @@ def tile_lstm_pa_t_kernel(tc, x, Wxi, bxi, Wxc, bxc, Wxo, bxo, out):
             )
             return value
 
+        state = {}
         o_value = {}
         tanh_state = {}
 
-        def gates(n):
-            state = []
+        def new_state(n):
             for half in range(HALVES):
                 i_value = gate_value(n, "i", half)
                 c_value = gate_value(n, "c", half)
-                state.append(values.tile([P, GROUP], F32, name="state", tag="state"))
+                state[n, half] = values.tile([P, GROUP], F32, name="state", tag="state")
                 nc.gpsimd.tensor_tensor(
-                    out=state[half][:], in0=c_value[:], in1=i_value[:], op=MULT
+                    out=state[n, half][:], in0=c_value[:], in1=i_value[:], op=MULT
                 )
+
+        def output_gate(n):
             for half in range(HALVES):
                 o_value[n, half] = gate_value(n, "o", half)
                 tanh_state[n, half] = values.tile(
                     [P, GROUP], F32, name="tanh_state", tag="tanh_state"
                 )
                 nc.scalar.activation(
-                    out=tanh_state[n, half][:], in_=state[half][:], func=ACT.Tanh
+                    out=tanh_state[n, half][:], in_=state[n, half][:], func=ACT.Tanh
                 )
 
         hidden = {}
@@ -255,7 +257,9 @@ def tile_lstm_pa_t_kernel(tc, x, Wxi, bxi, Wxc, bxc, Wxo, bxo, out):
                 quantise_x(n + 1)
             if 0 <= n - 1 < GROUPS:
                 output_product(n - 1)
+            if n < GROUPS:
+                new_state(n)
             if 0 <= n - 2 < GROUPS:
                 store_output(n - 2)
             if n < GROUPS:
-                gates(n)
+                output_gate(n)

@@ -22,7 +22,7 @@ GROUP = 512
 ROW_TILES = GROUP // P
 GROUPS = BATCH // GROUP
 HALVES = D_OUT // P
-PAIR_WORDS = K_PASS // 2
+PAIR_WORDS = D_IN // 2
 GATES = ("i", "c", "o")
 
 
@@ -34,7 +34,7 @@ def tile_lstm_pa_t_kernel(tc, x, Wxi, bxi, Wxc, bxc, Wxo, bxo, out):
 
     with ExitStack() as ctx:
         const = ctx.enter_context(tc.tile_pool(name="const", bufs=1))
-        x_pool = ctx.enter_context(tc.tile_pool(name="x_pool", bufs=GROUPS * PASSES))
+        x_pool = ctx.enter_context(tc.tile_pool(name="x_pool", bufs=GROUPS))
         operand = ctx.enter_context(tc.tile_pool(name="operand", bufs=2))
         values = ctx.enter_context(tc.tile_pool(name="values", bufs=2 * HALVES))
         result = ctx.enter_context(tc.tile_pool(name="result", bufs=4))
@@ -58,14 +58,11 @@ def tile_lstm_pa_t_kernel(tc, x, Wxi, bxi, Wxc, bxc, Wxo, bxo, out):
             )
 
         def load_x(n):
-            for g in range(PASSES):
-                x_sb[n, g] = x_pool.tile([P, ROW_TILES * K_PASS], BF16, name="x_sb", tag="x_sb")
-                nc.sync.dma_start(
-                    out=x_sb[n, g][:].rearrange("r (j k) -> r j k", j=ROW_TILES),
-                    in_=x[n * GROUP : (n + 1) * GROUP, g * K_PASS : (g + 1) * K_PASS].rearrange(
-                        "(r j) k -> r j k", j=ROW_TILES
-                    ),
-                )
+            x_sb[n] = x_pool.tile([P, ROW_TILES * D_IN], BF16, name="x_sb", tag="x_sb")
+            nc.sync.dma_start(
+                out=x_sb[n][:],
+                in_=x[n * GROUP : (n + 1) * GROUP, :].rearrange("(r j) k -> r (j k)", j=ROW_TILES),
+            )
 
         bias_rows = const.tile([P, P], BF16)
         nc.vector.memset(bias_rows[:], 0.0)
@@ -123,13 +120,13 @@ def tile_lstm_pa_t_kernel(tc, x, Wxi, bxi, Wxc, bxc, Wxo, bxo, out):
                 [P, PASSES * GROUP * PACK], BF16, name="x_grouped", tag="x_grouped", align_bytes=64
             )
             grouped_words = x_grouped[n][:].bitcast(F32)
+            words = x_sb[n][:].bitcast(F32)
             for g in range(PASSES):
-                words = x_sb[n, g][:].bitcast(F32)
                 for first in range(0, ROW_TILES, 2):
                     turned = turn_psum.tile([P, GROUP], F32, name="x_turned", tag="turned")
                     for u in range(2):
                         for j in (first, first + 1):
-                            start = j * PAIR_WORDS + u * P
+                            start = j * PAIR_WORDS + (2 * g + u) * P
                             nc.tensor.transpose(
                                 turned[:, (2 * u + j - first) * P : (2 * u + j - first + 1) * P],
                                 words[:, start : start + P],
@@ -200,13 +197,13 @@ def tile_lstm_pa_t_kernel(tc, x, Wxi, bxi, Wxc, bxc, Wxo, bxo, out):
 
         def output_gate(n):
             for half in range(HALVES):
-                o_value[n, half] = gate_value(n, "o", half)
                 tanh_state[n, half] = values.tile(
                     [P, GROUP], F32, name="tanh_state", tag="tanh_state"
                 )
                 nc.scalar.activation(
                     out=tanh_state[n, half][:], in_=state[n, half][:], func=ACT.Tanh
                 )
+                o_value[n, half] = gate_value(n, "o", half)
 
         hidden = {}
 

@@ -22,7 +22,7 @@ GROUP = 512
 ROW_TILES = GROUP // P
 GROUPS = BATCH // GROUP
 HALVES = D_OUT // P
-PAIR_WORDS = D_IN // 2
+PAIR_WORDS = K_PASS // 2
 GATES = ("i", "c", "o")
 
 
@@ -34,8 +34,8 @@ def tile_lstm_pa_t_kernel(tc, x, Wxi, bxi, Wxc, bxc, Wxo, bxo, out):
 
     with ExitStack() as ctx:
         const = ctx.enter_context(tc.tile_pool(name="const", bufs=1))
-        x_pool = ctx.enter_context(tc.tile_pool(name="x_pool", bufs=GROUPS))
-        operand = ctx.enter_context(tc.tile_pool(name="operand", bufs=2))
+        x_pool = ctx.enter_context(tc.tile_pool(name="x_pool", bufs=GROUPS * PASSES))
+        operand = ctx.enter_context(tc.tile_pool(name="operand", bufs=2 * PASSES))
         values = ctx.enter_context(tc.tile_pool(name="values", bufs=2 * HALVES))
         result = ctx.enter_context(tc.tile_pool(name="result", bufs=4))
         gate_psum = ctx.enter_context(tc.psum_pool(name="gate_psum", bufs=4))
@@ -58,24 +58,29 @@ def tile_lstm_pa_t_kernel(tc, x, Wxi, bxi, Wxc, bxc, Wxo, bxo, out):
             )
 
         def load_x(n):
-            x_sb[n] = x_pool.tile([P, ROW_TILES * D_IN], BF16, name="x_sb", tag="x_sb")
-            nc.sync.dma_start(
-                out=x_sb[n][:],
-                in_=x[n * GROUP : (n + 1) * GROUP, :].rearrange("(r j) k -> r (j k)", j=ROW_TILES),
-            )
+            for g in range(PASSES):
+                x_sb[n, g] = x_pool.tile([P, ROW_TILES * K_PASS], BF16, name="x_sb", tag="x_sb")
+                nc.sync.dma_start(
+                    out=x_sb[n, g][:].rearrange("r (j k) -> r j k", j=ROW_TILES),
+                    in_=x[n * GROUP : (n + 1) * GROUP, g * K_PASS : (g + 1) * K_PASS].rearrange(
+                        "(r j) k -> r j k", j=ROW_TILES
+                    ),
+                )
 
         bias_rows = const.tile([P, P], BF16)
         nc.vector.memset(bias_rows[:], 0.0)
 
-        for gate in GATES:
-            load_weight(gate)
+        load_weight("i")
+        load_weight("c")
         load_x(0)
         for row, gate in enumerate(GATES):
             nc.sync.dma_start(
                 out=bias_rows[HALVES * row : HALVES * (row + 1), :],
                 in_=biases[gate].rearrange("(h d) -> h d", h=HALVES),
             )
-        for n in range(1, GROUPS):
+        load_x(1)
+        load_weight("o")
+        for n in range(2, GROUPS):
             load_x(n)
 
         bias_cols = const.tile([P, len(GATES) * HALVES], F32)
@@ -89,11 +94,11 @@ def tile_lstm_pa_t_kernel(tc, x, Wxi, bxi, Wxc, bxc, Wxo, bxo, out):
         w_codes = {}
         w_scales = {}
 
-        def regroup_weight(gate, copy):
+        def regroup_weight(gate):
             w_grouped[gate] = const.tile(
                 [P, PASSES * D_OUT * PACK], BF16, name="w_grouped_" + gate, align_bytes=64
             )
-            copy(
+            nc.vector.tensor_copy(
                 out=w_grouped[gate][:].rearrange("p (g c t) -> p g c t", g=PASSES, t=PACK),
                 in_=w_raw[gate][:].rearrange("p (g t c) -> p g c t", g=PASSES, t=PACK),
             )
@@ -115,59 +120,59 @@ def tile_lstm_pa_t_kernel(tc, x, Wxi, bxi, Wxc, bxc, Wxo, bxo, out):
         x_codes = {}
         x_scales = {}
 
-        def transpose_x(n):
-            x_grouped[n] = operand.tile(
-                [P, PASSES * GROUP * PACK], BF16, name="x_grouped", tag="x_grouped", align_bytes=64
-            )
-            grouped_words = x_grouped[n][:].bitcast(F32)
-            words = x_sb[n][:].bitcast(F32)
-            for g in range(PASSES):
-                for first in range(0, ROW_TILES, 2):
-                    turned = turn_psum.tile([P, GROUP], F32, name="x_turned", tag="turned")
-                    for u in range(2):
-                        for j in (first, first + 1):
-                            start = j * PAIR_WORDS + (2 * g + u) * P
-                            nc.tensor.transpose(
-                                turned[:, (2 * u + j - first) * P : (2 * u + j - first + 1) * P],
-                                words[:, start : start + P],
-                                identity[:],
-                            )
-                    start = (g * GROUP + first * P) * 2
-                    last = g == PASSES - 1 and first == ROW_TILES - 2
-                    copy = nc.scalar.copy if last else nc.vector.tensor_copy
-                    copy(
-                        out=grouped_words[:, start : start + GROUP].rearrange(
-                            "p (c u) -> p c u", u=2
-                        ),
-                        in_=turned[:].rearrange("p (u c) -> p c u", u=2),
-                    )
+        def empty_bank(turned_view, sbuf_view, on_scalar):
+            if on_scalar:
+                nc.scalar.copy(out=sbuf_view, in_=turned_view)
+            else:
+                nc.vector.tensor_copy(out=sbuf_view, in_=turned_view)
 
-        def quantise_x(n):
-            x_codes[n] = operand.tile(
-                [P, PASSES * GROUP], U32, name="x_codes", tag="x_codes", align_bytes=64
+        def transpose_x(n, g, scalar_banks):
+            x_grouped[n, g] = operand.tile(
+                [P, GROUP * PACK], BF16, name="x_grouped", tag="x_grouped", align_bytes=64
             )
-            x_scales[n] = operand.tile(
-                [P, PASSES * GROUP], U8, name="x_scales", tag="x_scales", align_bytes=64
-            )
-            for g in range(PASSES):
-                cols = slice(g * GROUP, (g + 1) * GROUP)
-                nc.vector.quantize_mx(
-                    out=x_codes[n][:, cols].bitcast(FP8X4),
-                    scales=x_scales[n][:, cols],
-                    in_=x_grouped[n][:, g * GROUP * PACK : (g + 1) * GROUP * PACK],
+            grouped_words = x_grouped[n, g][:].bitcast(F32)
+            words = x_sb[n, g][:].bitcast(F32)
+            for first in range(0, ROW_TILES, 2):
+                turned = turn_psum.tile([P, GROUP], F32, name="x_turned", tag="turned")
+                for u in range(2):
+                    for j in (first, first + 1):
+                        start = j * PAIR_WORDS + u * P
+                        nc.tensor.transpose(
+                            turned[:, (2 * u + j - first) * P : (2 * u + j - first + 1) * P],
+                            words[:, start : start + P],
+                            identity[:],
+                        )
+                empty_bank(
+                    turned[:].rearrange("p (u c) -> p c u", u=2),
+                    grouped_words[:, first * P * 2 : (first + 2) * P * 2].rearrange(
+                        "p (c u) -> p c u", u=2
+                    ),
+                    on_scalar=first >= ROW_TILES - 2 * scalar_banks,
                 )
+
+        def quantise_x(n, g):
+            x_codes[n, g] = operand.tile(
+                [P, GROUP], U32, name="x_codes", tag="x_codes", align_bytes=64
+            )
+            x_scales[n, g] = operand.tile(
+                [P, GROUP], U8, name="x_scales", tag="x_scales", align_bytes=64
+            )
+            nc.vector.quantize_mx(
+                out=x_codes[n, g][:].bitcast(FP8X4),
+                scales=x_scales[n, g][:],
+                in_=x_grouped[n, g][:],
+            )
 
         def gate_value(n, gate, half):
             acc = gate_psum.tile([P, GROUP], F32, name="acc", tag="acc")
             for g in range(PASSES):
                 w_cols = slice(g * D_OUT + half * P, g * D_OUT + (half + 1) * P)
-                x_cols = slice(g * GROUP, (g + 1) * GROUP)
                 nc.tensor.matmul_mx(
                     out=acc[:],
                     lhsT=w_codes[gate][:, w_cols].bitcast(FP8X4),
                     lhsT_scale=w_scales[gate][:, w_cols],
-                    rhs=x_codes[n][:, x_cols].bitcast(FP8X4),
-                    rhs_scale=x_scales[n][:, x_cols],
+                    rhs=x_codes[n, g][:].bitcast(FP8X4),
+                    rhs_scale=x_scales[n, g][:],
                     start=(g == 0),
                     stop=(g == PASSES - 1),
                 )
@@ -218,7 +223,7 @@ def tile_lstm_pa_t_kernel(tc, x, Wxi, bxi, Wxc, bxc, Wxo, bxo, out):
                     op=MULT,
                 )
 
-        def store_output(n):
+        def store_output(n, scalar_banks):
             group_rows = out[n * GROUP : (n + 1) * GROUP, :].rearrange(
                 "(r j) d -> r j d", j=ROW_TILES
             )
@@ -233,30 +238,37 @@ def tile_lstm_pa_t_kernel(tc, x, Wxi, bxi, Wxc, bxc, Wxo, bxo, out):
                             identity[:],
                         )
                 rows = result.tile([P, 2 * D_OUT], F32, name="rows", tag="rows")
-                nc.vector.tensor_copy(out=rows[:], in_=turned[:])
+                empty_bank(turned[:], rows[:], on_scalar=first >= ROW_TILES - 2 * scalar_banks)
                 nc.sync.dma_start(
                     out=group_rows[:, first : first + 2, :],
                     in_=rows[:].rearrange("r (j d) -> r j d", j=2),
                 )
 
-        regroup_weight("i", nc.vector.tensor_copy)
-        regroup_weight("c", nc.vector.tensor_copy)
-        regroup_weight("o", nc.scalar.copy)
+        regroup_weight("i")
+        regroup_weight("c")
         quantise_weight("i")
         quantise_weight("c")
-        transpose_x(0)
+        for g in range(PASSES):
+            transpose_x(0, g, scalar_banks=2)
         turn_biases()
-        quantise_x(0)
+        for g in range(PASSES):
+            quantise_x(0, g)
+        regroup_weight("o")
         quantise_weight("o")
         for n in range(GROUPS + 2):
             if n + 1 < GROUPS:
-                transpose_x(n + 1)
-                quantise_x(n + 1)
+                transpose_x(n + 1, 0, scalar_banks=0)
             if 0 <= n - 1 < GROUPS:
                 output_product(n - 1)
+            if n + 1 < GROUPS:
+                quantise_x(n + 1, 0)
             if n < GROUPS:
                 new_state(n)
+            if n + 1 < GROUPS:
+                transpose_x(n + 1, 1, scalar_banks=1)
             if 0 <= n - 2 < GROUPS:
-                store_output(n - 2)
+                store_output(n - 2, scalar_banks=(1 if n >= GROUPS else 0))
+            if n + 1 < GROUPS:
+                quantise_x(n + 1, 1)
             if n < GROUPS:
                 output_gate(n)

from contextlib import ExitStack

import concourse.mybir as mybir
from concourse.masks import make_identity

F32 = mybir.dt.float32
BF16 = mybir.dt.bfloat16
U32 = mybir.dt.uint32
U8 = mybir.dt.uint8
FP8X4 = mybir.dt.float8_e4m3fn_x4
ACT = mybir.ActivationFunctionType
MULT = mybir.AluOpType.mult

BATCH, D_IN, D_OUT = 4096, 1024, 256
FLOPS = 2 * BATCH * D_IN * 3 * D_OUT

P = 128
PACK = 4
K_PASS = P * PACK
PASSES = D_IN // K_PASS
GROUP = 512
ROW_TILES = GROUP // P
GROUPS = BATCH // GROUP
HALVES = D_OUT // P
PAIR_WORDS = K_PASS // 2
GATES = ("i", "c", "o")


def tile_lstm_pa_t_kernel(tc, x, Wxi, bxi, Wxc, bxc, Wxo, bxo, out):
    nc = tc.nc
    weights = {"i": Wxi, "c": Wxc, "o": Wxo}
    biases = {"i": bxi, "c": bxc, "o": bxo}
    functions = {"i": ACT.Sigmoid, "c": ACT.Tanh, "o": ACT.Sigmoid}

    with ExitStack() as ctx:
        const = ctx.enter_context(tc.tile_pool(name="const", bufs=1))
        x_pool = ctx.enter_context(tc.tile_pool(name="x_pool", bufs=GROUPS * PASSES))
        operand = ctx.enter_context(tc.tile_pool(name="operand", bufs=2 * PASSES))
        values = ctx.enter_context(tc.tile_pool(name="values", bufs=2 * HALVES))
        result = ctx.enter_context(tc.tile_pool(name="result", bufs=4))
        gate_psum = ctx.enter_context(tc.psum_pool(name="gate_psum", bufs=4))
        turn_psum = ctx.enter_context(tc.psum_pool(name="turn_psum", bufs=4))
        ctx.enter_context(tc.manual_schedule())

        identity = const.tile([P, P], F32)
        make_identity(nc, identity[:])
        identity_bf16 = const.tile([P, P], BF16)
        make_identity(nc, identity_bf16[:])

        w_raw = {}
        x_sb = {}

        def load_weight(gate):
            w_raw[gate] = const.tile([P, PASSES * PACK * D_OUT], BF16, name="w_raw_" + gate)
            nc.sync.dma_start(
                out=w_raw[gate][:].rearrange("p (s r) -> p s r", s=2 * PASSES),
                in_=weights[gate].rearrange("(s p e) c -> p s (e c)", p=P, e=2),
            )

        def load_x(n):
            for g in range(PASSES):
                x_sb[n, g] = x_pool.tile([P, ROW_TILES * K_PASS], BF16, name="x_sb", tag="x_sb")
                nc.sync.dma_start(
                    out=x_sb[n, g][:].rearrange("r (j k) -> r j k", j=ROW_TILES),
                    in_=x[n * GROUP : (n + 1) * GROUP, g * K_PASS : (g + 1) * K_PASS].rearrange(
                        "(r j) k -> r j k", j=ROW_TILES
                    ),
                )

        bias_rows = const.tile([P, P], BF16)
        nc.vector.memset(bias_rows[:], 0.0)

        load_weight("i")
        load_weight("c")
        load_x(0)
        for row, gate in enumerate(GATES):
            nc.sync.dma_start(
                out=bias_rows[HALVES * row : HALVES * (row + 1), :],
                in_=biases[gate].rearrange("(h d) -> h d", h=HALVES),
            )
        load_x(1)
        load_weight("o")
        for n in range(2, GROUPS):
            load_x(n)

        bias_cols = const.tile([P, len(GATES) * HALVES], F32)

        def turn_biases():
            bias_turned = turn_psum.tile([P, P], BF16, name="bias_turned", tag="turned")
            nc.tensor.transpose(bias_turned[:], bias_rows[:], identity_bf16[:])
            nc.scalar.copy(out=bias_cols[:], in_=bias_turned[:, 0 : len(GATES) * HALVES])

        w_grouped = {}
        w_codes = {}
        w_scales = {}

        def regroup_weight(gate):
            w_grouped[gate] = const.tile(
                [P, PASSES * D_OUT * PACK], BF16, name="w_grouped_" + gate, align_bytes=64
            )
            nc.vector.tensor_copy(
                out=w_grouped[gate][:].rearrange("p (g c t) -> p g c t", g=PASSES, t=PACK),
                in_=w_raw[gate][:].rearrange("p (g t c) -> p g c t", g=PASSES, t=PACK),
            )

        def quantise_weight(gate):
            w_codes[gate] = const.tile(
                [P, PASSES * D_OUT], U32, name="w_codes_" + gate, align_bytes=64
            )
            w_scales[gate] = const.tile(
                [P, PASSES * D_OUT], U8, name="w_scales_" + gate, align_bytes=64
            )
            nc.vector.quantize_mx(
                out=w_codes[gate][:].bitcast(FP8X4),
                scales=w_scales[gate][:],
                in_=w_grouped[gate][:],
            )

        x_grouped = {}
        x_codes = {}
        x_scales = {}

        def empty_bank(turned_view, sbuf_view, on_scalar):
            if on_scalar:
                nc.scalar.copy(out=sbuf_view, in_=turned_view)
            else:
                nc.vector.tensor_copy(out=sbuf_view, in_=turned_view)

        def transpose_x(n, g, scalar_banks):
            x_grouped[n, g] = operand.tile(
                [P, GROUP * PACK], BF16, name="x_grouped", tag="x_grouped", align_bytes=64
            )
            grouped_words = x_grouped[n, g][:].bitcast(F32)
            words = x_sb[n, g][:].bitcast(F32)
            for first in range(0, ROW_TILES, 2):
                turned = turn_psum.tile([P, GROUP], F32, name="x_turned", tag="turned")
                for u in range(2):
                    for j in (first, first + 1):
                        start = j * PAIR_WORDS + u * P
                        nc.tensor.transpose(
                            turned[:, (2 * u + j - first) * P : (2 * u + j - first + 1) * P],
                            words[:, start : start + P],
                            identity[:],
                        )
                empty_bank(
                    turned[:].rearrange("p (u c) -> p c u", u=2),
                    grouped_words[:, first * P * 2 : (first + 2) * P * 2].rearrange(
                        "p (c u) -> p c u", u=2
                    ),
                    on_scalar=first >= ROW_TILES - 2 * scalar_banks,
                )

        def quantise_x(n, g):
            x_codes[n, g] = operand.tile(
                [P, GROUP], U32, name="x_codes", tag="x_codes", align_bytes=64
            )
            x_scales[n, g] = operand.tile(
                [P, GROUP], U8, name="x_scales", tag="x_scales", align_bytes=64
            )
            nc.vector.quantize_mx(
                out=x_codes[n, g][:].bitcast(FP8X4),
                scales=x_scales[n, g][:],
                in_=x_grouped[n, g][:],
            )

        def gate_value(n, gate, half):
            acc = gate_psum.tile([P, GROUP], F32, name="acc", tag="acc")
            for g in range(PASSES):
                w_cols = slice(g * D_OUT + half * P, g * D_OUT + (half + 1) * P)
                nc.tensor.matmul_mx(
                    out=acc[:],
                    lhsT=w_codes[gate][:, w_cols].bitcast(FP8X4),
                    lhsT_scale=w_scales[gate][:, w_cols],
                    rhs=x_codes[n, g][:].bitcast(FP8X4),
                    rhs_scale=x_scales[n, g][:],
                    start=(g == 0),
                    stop=(g == PASSES - 1),
                )
            value = values.tile([P, GROUP], F32, name="gate_" + gate, tag="gate_" + gate)
            column = GATES.index(gate) * HALVES + half
            nc.scalar.activation(
                out=value[:],
                in_=acc[:],
                func=functions[gate],
                bias=bias_cols[:, column : column + 1],
                scale=1.0,
            )
            return value

        state = {}
        o_value = {}
        tanh_state = {}

        def new_state(n):
            for half in range(HALVES):
                i_value = gate_value(n, "i", half)
                c_value = gate_value(n, "c", half)
                state[n, half] = values.tile([P, GROUP], F32, name="state", tag="state")
                nc.gpsimd.tensor_tensor(
                    out=state[n, half][:], in0=c_value[:], in1=i_value[:], op=MULT
                )

        def output_gate(n):
            for half in range(HALVES):
                tanh_state[n, half] = values.tile(
                    [P, GROUP], F32, name="tanh_state", tag="tanh_state"
                )
                nc.scalar.activation(
                    out=tanh_state[n, half][:], in_=state[n, half][:], func=ACT.Tanh
                )
                o_value[n, half] = gate_value(n, "o", half)

        hidden = {}

        def output_product(n):
            for half in range(HALVES):
                hidden[n, half] = values.tile([P, GROUP], F32, name="hidden", tag="hidden")
                engine = nc.vector if half == HALVES - 1 else nc.gpsimd
                engine.tensor_tensor(
                    out=hidden[n, half][:],
                    in0=tanh_state[n, half][:],
                    in1=o_value[n, half][:],
                    op=MULT,
                )

        def store_output(n, scalar_banks):
            group_rows = out[n * GROUP : (n + 1) * GROUP, :].rearrange(
                "(r j) d -> r j d", j=ROW_TILES
            )
            for first in range(0, ROW_TILES, 2):
                turned = turn_psum.tile([P, GROUP], F32, name="out_turned", tag="turned")
                for j in (first, first + 1):
                    for half in range(HALVES):
                        start = (j - first) * D_OUT + half * P
                        nc.tensor.transpose(
                            turned[:, start : start + P],
                            hidden[n, half][:, j * P : (j + 1) * P],
                            identity[:],
                        )
                rows = result.tile([P, 2 * D_OUT], F32, name="rows", tag="rows")
                empty_bank(turned[:], rows[:], on_scalar=first >= ROW_TILES - 2 * scalar_banks)
                nc.sync.dma_start(
                    out=group_rows[:, first : first + 2, :],
                    in_=rows[:].rearrange("r (j d) -> r j d", j=2),
                )

        regroup_weight("i")
        regroup_weight("c")
        quantise_weight("i")
        quantise_weight("c")
        for g in range(PASSES):
            transpose_x(0, g, scalar_banks=2)
        turn_biases()
        for g in range(PASSES):
            quantise_x(0, g)
        regroup_weight("o")
        quantise_weight("o")
        for n in range(GROUPS + 2):
            if n + 1 < GROUPS:
                transpose_x(n + 1, 0, scalar_banks=0)
            if 0 <= n - 1 < GROUPS:
                output_product(n - 1)
            if n + 1 < GROUPS:
                quantise_x(n + 1, 0)
            if n < GROUPS:
                new_state(n)
            if n + 1 < GROUPS:
                transpose_x(n + 1, 1, scalar_banks=1)
            if 0 <= n - 2 < GROUPS:
                store_output(n - 2, scalar_banks=(1 if n >= GROUPS else 0))
            if n + 1 < GROUPS:
                quantise_x(n + 1, 1)
            if n < GROUPS:
                output_gate(n)
